import numpy as np
import ml_dtypes


def mxq(x, axis, fmt="e4m3"):
    dtype, down = {"e4m3": (ml_dtypes.float8_e4m3fn, 7), "e5m2": (ml_dtypes.float8_e5m2, 14)}[fmt]
    v = np.moveaxis(np.asarray(x, np.float32).astype(ml_dtypes.bfloat16).astype(np.float64), axis, -1)
    blocks = v.reshape(v.shape[:-1] + (-1, 32))
    amax = np.abs(blocks).max(-1, keepdims=True)
    byte = np.maximum(np.where(amax > 0, np.frexp(amax)[1] - 1 + 127, 0) - down, 1)
    scale = np.exp2(byte - 127.0)
    codes = (blocks / scale).astype(np.float32).astype(dtype).astype(np.float64)
    return np.moveaxis((codes * scale).reshape(v.shape), -1, axis)


WIDE = False


def mx_kscale(k):
    if not WIDE:
        return np.ones(k)
    levels = np.array([10, -10, 5, -5, 0])
    a = np.random.permutation(np.resize(levels, k // 512 * 4)).reshape(k // 512, 4)
    idx = np.arange(k)
    return np.exp2(a[idx // 512, idx % 128 // 32])


BF16 = ml_dtypes.bfloat16


def bf(x):
    return np.asarray(x, np.float32).astype(BF16)


def f64(x):
    return np.asarray(x).astype(np.float64)


B, D, F = 8192, 512, 2560
EPS = 1e-12


def l2_gain_norm(h, g):
    n = np.sqrt((h * h).sum(-1, keepdims=True))
    return h / np.maximum(n, EPS) * (D ** -0.5) * g


def setup_inputs():
    s = mx_kscale(D)
    r = np.random.standard_normal
    return {"x": bf(r((B, D))),
            "state": bf(r((B, D))),
            "g1": bf(D * (1.0 + 0.1 * r(D)) * s),
            "wv": bf(r((D, D)) / np.sqrt(D) / s[None, :]),
            "bv": bf(0.2 * r(D))}


def reference(x, state, g1, wv, bv):
    h = f64(x) + f64(state)
    hn = l2_gain_norm(h, f64(g1))
    return (mxq(hn, 1, "e4m3") @ mxq(f64(wv), 1, "e4m3").T) + f64(bv)

@@ -1,0 +1,192 @@
+from contextlib import ExitStack
+
+import concourse.mybir as mybir
+from concourse.masks import make_identity
+
+F32 = mybir.dt.float32
+BF16 = mybir.dt.bfloat16
+U32 = mybir.dt.uint32
+U8 = mybir.dt.uint8
+FP8X4 = mybir.dt.float8_e4m3fn_x4
+ACT = mybir.ActivationFunctionType
+ALU = mybir.AluOpType
+
+P = 128
+PACK = 4
+D = P * PACK
+B = 8192
+EPS = 1e-12
+TILES = 4
+GROUP_ROWS = P * TILES
+GROUPS = B // GROUP_ROWS
+LOADS_AHEAD = 2
+
+FLOPS = 2 * B * D * D
+
+
+def tile_recurrenttransformerblock_pa_t_kernel(tc, x, state, g1, wv, bv, out):
+    nc = tc.nc
+
+    def group_view(dram, g):
+        rows = dram[g * GROUP_ROWS : (g + 1) * GROUP_ROWS, :]
+        return rows.rearrange("(p t) k -> p t k", t=TILES)
+
+    with ExitStack() as ctx:
+        const = ctx.enter_context(tc.tile_pool(name="const", bufs=1))
+        inputs = ctx.enter_context(tc.tile_pool(name="inputs", bufs=LOADS_AHEAD + 1))
+        sums = ctx.enter_context(tc.tile_pool(name="sums", bufs=3))
+        stats = ctx.enter_context(tc.tile_pool(name="stats", bufs=3))
+        scaled = ctx.enter_context(tc.tile_pool(name="scaled", bufs=2))
+        packed = ctx.enter_context(tc.tile_pool(name="packed", bufs=2))
+        results = ctx.enter_context(tc.tile_pool(name="results", bufs=3))
+        turned = ctx.enter_context(tc.psum_pool(name="turned", bufs=TILES))
+        products = ctx.enter_context(tc.psum_pool(name="products", bufs=TILES))
+        ctx.enter_context(tc.manual_schedule())
+
+        x_rows, s_rows, h, inv_norm, h_unit, h_turned = {}, {}, {}, {}, {}, {}
+        hn_words, hn_codes, hn_scales, v_sums = {}, {}, {}, {}
+
+        def load(g):
+            x_rows[g] = inputs.tile([P, TILES, D], BF16, name="x_rows")
+            s_rows[g] = inputs.tile([P, TILES, D], BF16, name="s_rows")
+            nc.sync.dma_start(out=x_rows[g][:], in_=group_view(x, g))
+            nc.sync.dma_start(out=s_rows[g][:], in_=group_view(state, g))
+
+        load(0)
+
+        ident_f32 = const.tile([P, P], F32)
+        make_identity(nc, ident_f32[:])
+        ident_bf16 = const.tile([P, P], BF16)
+        make_identity(nc, ident_bf16[:])
+
+        one = const.tile([P, 1], F32)
+        nc.vector.memset(one[:], 1.0)
+        warm = const.tile([P, 1], F32)
+        nc.scalar.activation(out=warm[:], in_=one[:], func=ACT.Abs_reciprocal_sqrt)
+
+        g_rows = const.tile([P, P], BF16)
+        nc.vector.memset(g_rows[:], 0.0)
+        nc.sync.dma_start(out=g_rows[0:PACK, :], in_=g1.rearrange("(c p) -> c p", p=P))
+        w_rows = const.tile([P, PACK, D], BF16)
+        nc.sync.dma_start(out=w_rows[:], in_=wv.rearrange("(b p) k -> p b k", p=P))
+        bias_rows = const.tile([P, D], BF16)
+        nc.sync.dma_start(out=bias_rows[:], in_=bv.partition_broadcast(P))
+        for g in range(1, LOADS_AHEAD):
+            load(g)
+
+        g_turned = turned.tile([P, PACK, P], BF16, tag="turned")
+        nc.tensor.transpose(g_turned[:, 0, :], g_rows[:], ident_bf16[:])
+        gain_by_k = const.tile([P, PACK], F32)
+        nc.vector.tensor_copy(out=gain_by_k[:], in_=g_turned[:, 0, 0:PACK])
+
+        w_words = const.tile([P, D, PACK], BF16, align_bytes=64)
+        for b in range(PACK):
+            w_turned = turned.tile([P, PACK, P], BF16, tag="turned")
+            for c in range(PACK):
+                nc.tensor.transpose(w_turned[:, c, :], w_rows[:, b, c * P : (c + 1) * P], ident_bf16[:])
+            nc.vector.tensor_copy(
+                out=w_words[:, b * P : (b + 1) * P, :], in_=w_turned[:].rearrange("p c n -> p n c")
+            )
+        w_codes = const.tile([P, D], U32, align_bytes=64)
+        w_scales = const.tile([P, D], U8, align_bytes=64)
+        nc.vector.quantize_mx(
+            out=w_codes[:].bitcast(FP8X4), scales=w_scales[:], in_=w_words[:].rearrange("p n c -> p (n c)")
+        )
+
+        squares = const.tile([P, D], F32)
+
+        def add_inputs(g):
+            h[g] = sums.tile([P, TILES, D], F32, name="h")
+            for t in range(TILES):
+                nc.gpsimd.tensor_tensor(
+                    out=h[g][:, t, :], in0=x_rows[g][:, t, :], in1=s_rows[g][:, t, :], op=ALU.add
+                )
+
+        def normalise(g):
+            sum_sq = stats.tile([P, TILES], F32, name="sum_sq")
+            for t in range(TILES):
+                nc.scalar.activation(
+                    out=squares[:], in_=h[g][:, t, :], func=ACT.Square, accum_out=sum_sq[:, t : t + 1]
+                )
+            excess = stats.tile([P, TILES], F32, name="excess")
+            nc.scalar.activation(out=excess[:], in_=sum_sq[:], func=ACT.Relu, bias=-EPS * EPS)
+            inv_norm[g] = stats.tile([P, TILES], F32, name="inv_norm")
+            nc.scalar.activation(
+                out=inv_norm[g][:],
+                in_=excess[:],
+                func=ACT.Abs_reciprocal_sqrt,
+                scale=float(D),
+                bias=float(D) * EPS * EPS,
+            )
+            h_unit[g] = scaled.tile([P, TILES, D], F32, name="h_unit")
+            for t in range(TILES):
+                nc.scalar.activation(
+                    out=h_unit[g][:, t, :], in_=h[g][:, t, :], func=ACT.Copy, scale=inv_norm[g][:, t : t + 1]
+                )
+
+        def transpose(g):
+            h_turned[g] = []
+            for t in range(TILES):
+                bank = turned.tile([P, PACK, P], F32, tag="turned", name="h_turned")
+                for c in range(PACK):
+                    nc.tensor.transpose(bank[:, c, :], h_unit[g][:, t, c * P : (c + 1) * P], ident_f32[:])
+                h_turned[g].append(bank)
+
+        def apply_gain(g):
+            hn_words[g] = packed.tile([P, TILES, P, PACK], BF16, name="hn_words", align_bytes=64)
+            for t in range(TILES):
+                nc.vector.tensor_tensor(
+                    out=hn_words[g][:, t, :, :],
+                    in0=h_turned[g][t][:].rearrange("p c r -> p r c"),
+                    in1=gain_by_k[:].unsqueeze(1).to_broadcast([P, P, PACK]),
+                    op=ALU.mult,
+                )
+
+        def quantise(g):
+            hn_codes[g] = packed.tile([P, TILES * P], U32, name="hn_codes", align_bytes=64)
+            hn_scales[g] = packed.tile([P, TILES * P], U8, name="hn_scales", align_bytes=64)
+            nc.vector.quantize_mx(
+                out=hn_codes[g][:].bitcast(FP8X4),
+                scales=hn_scales[g][:],
+                in_=hn_words[g][:].rearrange("p t r c -> p (t r c)"),
+            )
+
+        def multiply(g):
+            v_sums[g] = []
+            for t in range(TILES):
+                acc = products.tile([P, D], F32, tag="products", name="v_sums")
+                nc.tensor.matmul_mx(
+                    out=acc[:],
+                    lhsT=hn_codes[g][:, t * P : (t + 1) * P].bitcast(FP8X4),
+                    lhsT_scale=hn_scales[g][:, t * P : (t + 1) * P],
+                    rhs=w_codes[:].bitcast(FP8X4),
+                    rhs_scale=w_scales[:],
+                    start=True,
+                    stop=True,
+                )
+                v_sums[g].append(acc)
+
+        def add_bias_and_store(g):
+            v = results.tile([P, TILES, D], F32, name="v")
+            for t in range(TILES):
+                nc.vector.tensor_tensor(out=v[:, t, :], in0=v_sums[g][t][:], in1=bias_rows[:], op=ALU.add)
+            nc.sync.dma_start(out=group_view(out, g), in_=v[:])
+
+        def due(g):
+            return 0 <= g < GROUPS
+
+        for j in range(GROUPS + 3):
+            if due(j + LOADS_AHEAD):
+                load(j + LOADS_AHEAD)
+            if due(j):
+                add_inputs(j)
+            if due(j - 3):
+                quantise(j - 3)
+                multiply(j - 3)
+            if due(j - 1):
+                normalise(j - 1)
+                transpose(j - 1)
+            if due(j - 2):
+                apply_gain(j - 2)
+            if due(j - 3):
+                add_bias_and_store(j - 3)

@@ -20,6 +20,7 @@ TILES = 4
 GROUP_ROWS = P * TILES
 GROUPS = B // GROUP_ROWS
 LOADS_AHEAD = 2
+ADD_TILES = 2
 
 FLOPS = 2 * B * D * D
 
@@ -97,9 +98,10 @@ def tile_recurrenttransformerblock_pa_t_kernel(tc, x, state, g1, wv, bv, out):
 
         def add_inputs(g):
             h[g] = sums.tile([P, TILES, D], F32, name="h")
-            for t in range(TILES):
+            for t in range(0, TILES, ADD_TILES):
+                part = slice(t, t + ADD_TILES)
                 nc.gpsimd.tensor_tensor(
-                    out=h[g][:, t, :], in0=x_rows[g][:, t, :], in1=s_rows[g][:, t, :], op=ALU.add
+                    out=h[g][:, part, :], in0=x_rows[g][:, part, :], in1=s_rows[g][:, part, :], op=ALU.add
                 )
 
         def normalise(g):

@@ -20,7 +20,7 @@ TILES = 4
 GROUP_ROWS = P * TILES
 GROUPS = B // GROUP_ROWS
 LOADS_AHEAD = 2
-ADD_TILES = 2
+ADD_TILES = 4
 
 FLOPS = 2 * B * D * D
 

@@ -20,7 +20,7 @@ TILES = 4
 GROUP_ROWS = P * TILES
 GROUPS = B // GROUP_ROWS
 LOADS_AHEAD = 2
-ADD_TILES = 4
+ADD_TILES = 2
 
 FLOPS = 2 * B * D * D
 
@@ -44,7 +44,7 @@ def tile_recurrenttransformerblock_pa_t_kernel(tc, x, state, g1, wv, bv, out):
         products = ctx.enter_context(tc.psum_pool(name="products", bufs=TILES))
         ctx.enter_context(tc.manual_schedule())
 
-        x_rows, s_rows, h, inv_norm, h_unit, h_turned = {}, {}, {}, {}, {}, {}
+        x_rows, s_rows, h, sum_sq, excess, inv_norm, h_unit, h_turned = {}, {}, {}, {}, {}, {}, {}, {}
         hn_words, hn_codes, hn_scales, v_sums = {}, {}, {}, {}
 
         def load(g):
@@ -104,24 +104,29 @@ def tile_recurrenttransformerblock_pa_t_kernel(tc, x, state, g1, wv, bv, out):
                     out=h[g][:, part, :], in0=x_rows[g][:, part, :], in1=s_rows[g][:, part, :], op=ALU.add
                 )
 
-        def normalise(g):
-            sum_sq = stats.tile([P, TILES], F32, name="sum_sq")
+        def sum_squares(g):
+            sum_sq[g] = stats.tile([P, TILES], F32, name="sum_sq")
             for t in range(TILES):
                 nc.scalar.activation(
-                    out=squares[:], in_=h[g][:, t, :], func=ACT.Square, accum_out=sum_sq[:, t : t + 1]
+                    out=squares[:], in_=h[g][:, t, :], func=ACT.Square, accum_out=sum_sq[g][:, t : t + 1]
                 )
-            excess = stats.tile([P, TILES], F32, name="excess")
-            nc.scalar.activation(out=excess[:], in_=sum_sq[:], func=ACT.Relu, bias=-EPS * EPS)
+
+        def clamp(g):
+            excess[g] = stats.tile([P, TILES], F32, name="excess")
+            nc.scalar.activation(out=excess[g][:], in_=sum_sq[g][:], func=ACT.Relu, bias=-EPS * EPS)
+
+        def invert(g):
             inv_norm[g] = stats.tile([P, TILES], F32, name="inv_norm")
             nc.scalar.activation(
                 out=inv_norm[g][:],
-                in_=excess[:],
+                in_=excess[g][:],
                 func=ACT.Abs_reciprocal_sqrt,
                 scale=float(D),
                 bias=float(D) * EPS * EPS,
             )
-            h_unit[g] = scaled.tile([P, TILES, D], F32, name="h_unit")
-            for t in range(TILES):
+
+        def scale_rows(g, tiles):
+            for t in tiles:
                 nc.scalar.activation(
                     out=h_unit[g][:, t, :], in_=h[g][:, t, :], func=ACT.Copy, scale=inv_norm[g][:, t : t + 1]
                 )
@@ -177,18 +182,28 @@ def tile_recurrenttransformerblock_pa_t_kernel(tc, x, state, g1, wv, bv, out):
         def due(g):
             return 0 <= g < GROUPS
 
-        for j in range(GROUPS + 3):
+        for j in range(GROUPS + 4):
             if due(j + LOADS_AHEAD):
                 load(j + LOADS_AHEAD)
             if due(j):
                 add_inputs(j)
-            if due(j - 3):
-                quantise(j - 3)
-                multiply(j - 3)
+            if due(j - 4):
+                quantise(j - 4)
+                multiply(j - 4)
             if due(j - 1):
-                normalise(j - 1)
-                transpose(j - 1)
+                sum_squares(j - 1)
             if due(j - 2):
-                apply_gain(j - 2)
+                h_unit[j - 2] = scaled.tile([P, TILES, D], F32, name="h_unit")
+                scale_rows(j - 2, range(0, TILES // 2))
+            if due(j - 1):
+                clamp(j - 1)
+            if due(j - 2):
+                scale_rows(j - 2, range(TILES // 2, TILES))
+            if due(j - 1):
+                invert(j - 1)
+            if due(j - 2):
+                transpose(j - 2)
             if due(j - 3):
-                add_bias_and_store(j - 3)
+                apply_gain(j - 3)
+            if due(j - 4):
+                add_bias_and_store(j - 4)

@@ -19,8 +19,10 @@ EPS = 1e-12
 TILES = 4
 GROUP_ROWS = P * TILES
 GROUPS = B // GROUP_ROWS
-LOADS_AHEAD = 2
+LOADS_AHEAD = 4
 ADD_TILES = 2
+VECTOR_ADDS = 3
+STORE_TILES = 2
 
 FLOPS = 2 * B * D * D
 
@@ -53,7 +55,8 @@ def tile_recurrenttransformerblock_pa_t_kernel(tc, x, state, g1, wv, bv, out):
             nc.sync.dma_start(out=x_rows[g][:], in_=group_view(x, g))
             nc.sync.dma_start(out=s_rows[g][:], in_=group_view(state, g))
 
-        load(0)
+        for g in range(LOADS_AHEAD):
+            load(g)
 
         ident_f32 = const.tile([P, P], F32)
         make_identity(nc, ident_f32[:])
@@ -72,8 +75,19 @@ def tile_recurrenttransformerblock_pa_t_kernel(tc, x, state, g1, wv, bv, out):
         nc.sync.dma_start(out=w_rows[:], in_=wv.rearrange("(b p) k -> p b k", p=P))
         bias_rows = const.tile([P, D], BF16)
         nc.sync.dma_start(out=bias_rows[:], in_=bv.partition_broadcast(P))
-        for g in range(1, LOADS_AHEAD):
-            load(g)
+        squares = const.tile([P, D], F32)
+
+        def add_inputs(g):
+            engine = nc.vector if g < VECTOR_ADDS else nc.gpsimd
+            h[g] = sums.tile([P, TILES, D], F32, name="h")
+            for t in range(0, TILES, ADD_TILES):
+                part = slice(t, t + ADD_TILES)
+                engine.tensor_tensor(
+                    out=h[g][:, part, :], in0=x_rows[g][:, part, :], in1=s_rows[g][:, part, :], op=ALU.add
+                )
+
+        for g in range(VECTOR_ADDS):
+            add_inputs(g)
 
         g_turned = turned.tile([P, PACK, P], BF16, tag="turned")
         nc.tensor.transpose(g_turned[:, 0, :], g_rows[:], ident_bf16[:])
@@ -93,16 +107,6 @@ def tile_recurrenttransformerblock_pa_t_kernel(tc, x, state, g1, wv, bv, out):
         nc.vector.quantize_mx(
             out=w_codes[:].bitcast(FP8X4), scales=w_scales[:], in_=w_words[:].rearrange("p n c -> p (n c)")
         )
-
-        squares = const.tile([P, D], F32)
-
-        def add_inputs(g):
-            h[g] = sums.tile([P, TILES, D], F32, name="h")
-            for t in range(0, TILES, ADD_TILES):
-                part = slice(t, t + ADD_TILES)
-                nc.gpsimd.tensor_tensor(
-                    out=h[g][:, part, :], in0=x_rows[g][:, part, :], in1=s_rows[g][:, part, :], op=ALU.add
-                )
 
         def sum_squares(g):
             sum_sq[g] = stats.tile([P, TILES], F32, name="sum_sq")
@@ -177,7 +181,9 @@ def tile_recurrenttransformerblock_pa_t_kernel(tc, x, state, g1, wv, bv, out):
             v = results.tile([P, TILES, D], F32, name="v")
             for t in range(TILES):
                 nc.vector.tensor_tensor(out=v[:, t, :], in0=v_sums[g][t][:], in1=bias_rows[:], op=ALU.add)
-            nc.sync.dma_start(out=group_view(out, g), in_=v[:])
+                if (t + 1) % STORE_TILES == 0:
+                    part = slice(t + 1 - STORE_TILES, t + 1)
+                    nc.sync.dma_start(out=group_view(out, g)[:, part, :], in_=v[:, part, :])
 
         def due(g):
             return 0 <= g < GROUPS
@@ -185,7 +191,7 @@ def tile_recurrenttransformerblock_pa_t_kernel(tc, x, state, g1, wv, bv, out):
         for j in range(GROUPS + 4):
             if due(j + LOADS_AHEAD):
                 load(j + LOADS_AHEAD)
-            if due(j):
+            if VECTOR_ADDS <= j < GROUPS:
                 add_inputs(j)
             if due(j - 4):
                 quantise(j - 4)

@@ -78,10 +78,10 @@ def tile_recurrenttransformerblock_pa_t_kernel(tc, x, state, g1, wv, bv, out):
         squares = const.tile([P, D], F32)
 
         def add_inputs(g):
-            engine = nc.vector if g < VECTOR_ADDS else nc.gpsimd
+            engine, step = (nc.vector, ADD_TILES) if g < VECTOR_ADDS else (nc.gpsimd, TILES)
             h[g] = sums.tile([P, TILES, D], F32, name="h")
-            for t in range(0, TILES, ADD_TILES):
-                part = slice(t, t + ADD_TILES)
+            for t in range(0, TILES, step):
+                part = slice(t, t + step)
                 engine.tensor_tensor(
                     out=h[g][:, part, :], in0=x_rows[g][:, part, :], in1=s_rows[g][:, part, :], op=ALU.add
                 )

@@ -24,6 +24,10 @@ ADD_TILES = 2
 VECTOR_ADDS = 3
 STORE_TILES = 2
 
+NORMALISE_LAG = 1
+GAIN_LAG = 2
+PRODUCT_LAG = 3
+
 FLOPS = 2 * B * D * D
 
 
@@ -39,9 +43,9 @@ def tile_recurrenttransformerblock_pa_t_kernel(tc, x, state, g1, wv, bv, out):
         inputs = ctx.enter_context(tc.tile_pool(name="inputs", bufs=LOADS_AHEAD + 1))
         sums = ctx.enter_context(tc.tile_pool(name="sums", bufs=3))
         stats = ctx.enter_context(tc.tile_pool(name="stats", bufs=3))
+        results = ctx.enter_context(tc.tile_pool(name="results", bufs=3))
         scaled = ctx.enter_context(tc.tile_pool(name="scaled", bufs=2))
         packed = ctx.enter_context(tc.tile_pool(name="packed", bufs=2))
-        results = ctx.enter_context(tc.tile_pool(name="results", bufs=3))
         turned = ctx.enter_context(tc.psum_pool(name="turned", bufs=TILES))
         products = ctx.enter_context(tc.psum_pool(name="products", bufs=TILES))
         ctx.enter_context(tc.manual_schedule())
@@ -54,6 +58,15 @@ def tile_recurrenttransformerblock_pa_t_kernel(tc, x, state, g1, wv, bv, out):
             s_rows[g] = inputs.tile([P, TILES, D], BF16, name="s_rows")
             nc.sync.dma_start(out=x_rows[g][:], in_=group_view(x, g))
             nc.sync.dma_start(out=s_rows[g][:], in_=group_view(state, g))
+
+        def add_inputs(g):
+            engine = nc.vector if g < VECTOR_ADDS else nc.gpsimd
+            h[g] = sums.tile([P, TILES, D], F32, name="h")
+            for t in range(0, TILES, ADD_TILES):
+                part = slice(t, t + ADD_TILES)
+                engine.tensor_tensor(
+                    out=h[g][:, part, :], in0=x_rows[g][:, part, :], in1=s_rows[g][:, part, :], op=ALU.add
+                )
 
         for g in range(LOADS_AHEAD):
             load(g)
@@ -75,16 +88,6 @@ def tile_recurrenttransformerblock_pa_t_kernel(tc, x, state, g1, wv, bv, out):
         nc.sync.dma_start(out=w_rows[:], in_=wv.rearrange("(b p) k -> p b k", p=P))
         bias_rows = const.tile([P, D], BF16)
         nc.sync.dma_start(out=bias_rows[:], in_=bv.partition_broadcast(P))
-        squares = const.tile([P, D], F32)
-
-        def add_inputs(g):
-            engine, step = (nc.vector, ADD_TILES) if g < VECTOR_ADDS else (nc.gpsimd, TILES)
-            h[g] = sums.tile([P, TILES, D], F32, name="h")
-            for t in range(0, TILES, step):
-                part = slice(t, t + step)
-                engine.tensor_tensor(
-                    out=h[g][:, part, :], in0=x_rows[g][:, part, :], in1=s_rows[g][:, part, :], op=ALU.add
-                )
 
         for g in range(VECTOR_ADDS):
             add_inputs(g)
@@ -108,32 +111,46 @@ def tile_recurrenttransformerblock_pa_t_kernel(tc, x, state, g1, wv, bv, out):
             out=w_codes[:].bitcast(FP8X4), scales=w_scales[:], in_=w_words[:].rearrange("p n c -> p (n c)")
         )
 
-        def sum_squares(g):
-            sum_sq[g] = stats.tile([P, TILES], F32, name="sum_sq")
-            for t in range(TILES):
-                nc.scalar.activation(
-                    out=squares[:], in_=h[g][:, t, :], func=ACT.Square, accum_out=sum_sq[g][:, t : t + 1]
-                )
+        squares = const.tile([P, D], F32)
 
-        def clamp(g):
-            excess[g] = stats.tile([P, TILES], F32, name="excess")
-            nc.scalar.activation(out=excess[g][:], in_=sum_sq[g][:], func=ACT.Relu, bias=-EPS * EPS)
-
-        def invert(g):
-            inv_norm[g] = stats.tile([P, TILES], F32, name="inv_norm")
+        def sum_squares(g, t):
             nc.scalar.activation(
-                out=inv_norm[g][:],
-                in_=excess[g][:],
+                out=squares[:], in_=h[g][:, t, :], func=ACT.Square, accum_out=sum_sq[g][:, t : t + 1]
+            )
+
+        def clamp(g, t):
+            nc.scalar.activation(
+                out=excess[g][:, t : t + 1], in_=sum_sq[g][:, t : t + 1], func=ACT.Relu, bias=-EPS * EPS
+            )
+
+        def invert(g, t):
+            nc.scalar.activation(
+                out=inv_norm[g][:, t : t + 1],
+                in_=excess[g][:, t : t + 1],
                 func=ACT.Abs_reciprocal_sqrt,
                 scale=float(D),
                 bias=float(D) * EPS * EPS,
             )
 
-        def scale_rows(g, tiles):
-            for t in tiles:
-                nc.scalar.activation(
-                    out=h_unit[g][:, t, :], in_=h[g][:, t, :], func=ACT.Copy, scale=inv_norm[g][:, t : t + 1]
-                )
+        def scale_rows(g, t):
+            nc.scalar.activation(
+                out=h_unit[g][:, t, :], in_=h[g][:, t, :], func=ACT.Copy, scale=inv_norm[g][:, t : t + 1]
+            )
+
+        def normalise(g):
+            sum_sq[g] = stats.tile([P, TILES], F32, name="sum_sq")
+            excess[g] = stats.tile([P, TILES], F32, name="excess")
+            inv_norm[g] = stats.tile([P, TILES], F32, name="inv_norm")
+            h_unit[g] = scaled.tile([P, TILES, D], F32, name="h_unit")
+            for i in range(2 * TILES):
+                if i < TILES:
+                    sum_squares(g, i)
+                else:
+                    scale_rows(g, i - TILES)
+                if 1 <= i <= TILES:
+                    clamp(g, i - 1)
+                if 2 <= i <= TILES + 1:
+                    invert(g, i - 2)
 
         def transpose(g):
             h_turned[g] = []
@@ -188,28 +205,18 @@ def tile_recurrenttransformerblock_pa_t_kernel(tc, x, state, g1, wv, bv, out):
         def due(g):
             return 0 <= g < GROUPS
 
-        for j in range(GROUPS + 4):
+        for j in range(GROUPS + PRODUCT_LAG):
             if due(j + LOADS_AHEAD):
                 load(j + LOADS_AHEAD)
             if VECTOR_ADDS <= j < GROUPS:
                 add_inputs(j)
-            if due(j - 4):
-                quantise(j - 4)
-                multiply(j - 4)
-            if due(j - 1):
-                sum_squares(j - 1)
-            if due(j - 2):
-                h_unit[j - 2] = scaled.tile([P, TILES, D], F32, name="h_unit")
-                scale_rows(j - 2, range(0, TILES // 2))
-            if due(j - 1):
-                clamp(j - 1)
-            if due(j - 2):
-                scale_rows(j - 2, range(TILES // 2, TILES))
-            if due(j - 1):
-                invert(j - 1)
-            if due(j - 2):
-                transpose(j - 2)
-            if due(j - 3):
-                apply_gain(j - 3)
-            if due(j - 4):
-                add_bias_and_store(j - 4)
+            if due(j - PRODUCT_LAG):
+                quantise(j - PRODUCT_LAG)
+                multiply(j - PRODUCT_LAG)
+            if due(j - NORMALISE_LAG):
+                normalise(j - NORMALISE_LAG)
+                transpose(j - NORMALISE_LAG)
+            if due(j - GAIN_LAG):
+                apply_gain(j - GAIN_LAG)
+            if due(j - PRODUCT_LAG):
+                add_bias_and_store(j - PRODUCT_LAG)

from contextlib import ExitStack

import concourse.mybir as mybir
from concourse.masks import make_identity

F32 = mybir.dt.float32
BF16 = mybir.dt.bfloat16
U32 = mybir.dt.uint32
U8 = mybir.dt.uint8
FP8X4 = mybir.dt.float8_e4m3fn_x4
ACT = mybir.ActivationFunctionType
ALU = mybir.AluOpType

P = 128
PACK = 4
D = P * PACK
B = 8192
EPS = 1e-12
TILES = 4
GROUP_ROWS = P * TILES
GROUPS = B // GROUP_ROWS
LOADS_AHEAD = 4
ADD_TILES = 2
VECTOR_ADDS = 3
STORE_TILES = 2

NORMALISE_LAG = 1
GAIN_LAG = 2
PRODUCT_LAG = 3

FLOPS = 2 * B * D * D


def tile_recurrenttransformerblock_pa_t_kernel(tc, x, state, g1, wv, bv, out):
    nc = tc.nc

    def group_view(dram, g):
        rows = dram[g * GROUP_ROWS : (g + 1) * GROUP_ROWS, :]
        return rows.rearrange("(p t) k -> p t k", t=TILES)

    with ExitStack() as ctx:
        const = ctx.enter_context(tc.tile_pool(name="const", bufs=1))
        inputs = ctx.enter_context(tc.tile_pool(name="inputs", bufs=LOADS_AHEAD + 1))
        sums = ctx.enter_context(tc.tile_pool(name="sums", bufs=3))
        stats = ctx.enter_context(tc.tile_pool(name="stats", bufs=3))
        results = ctx.enter_context(tc.tile_pool(name="results", bufs=3))
        scaled = ctx.enter_context(tc.tile_pool(name="scaled", bufs=2))
        packed = ctx.enter_context(tc.tile_pool(name="packed", bufs=2))
        turned = ctx.enter_context(tc.psum_pool(name="turned", bufs=TILES))
        products = ctx.enter_context(tc.psum_pool(name="products", bufs=TILES))
        ctx.enter_context(tc.manual_schedule())

        x_rows, s_rows, h, sum_sq, excess, inv_norm, h_unit, h_turned = {}, {}, {}, {}, {}, {}, {}, {}
        hn_words, hn_codes, hn_scales, v_sums = {}, {}, {}, {}

        def load(g):
            x_rows[g] = inputs.tile([P, TILES, D], BF16, name="x_rows")
            s_rows[g] = inputs.tile([P, TILES, D], BF16, name="s_rows")
            nc.sync.dma_start(out=x_rows[g][:], in_=group_view(x, g))
            nc.sync.dma_start(out=s_rows[g][:], in_=group_view(state, g))

        def add_inputs(g):
            engine = nc.vector if g < VECTOR_ADDS else nc.gpsimd
            h[g] = sums.tile([P, TILES, D], F32, name="h")
            for t in range(0, TILES, ADD_TILES):
                part = slice(t, t + ADD_TILES)
                engine.tensor_tensor(
                    out=h[g][:, part, :], in0=x_rows[g][:, part, :], in1=s_rows[g][:, part, :], op=ALU.add
                )

        for g in range(LOADS_AHEAD):
            load(g)

        ident_f32 = const.tile([P, P], F32)
        make_identity(nc, ident_f32[:])
        ident_bf16 = const.tile([P, P], BF16)
        make_identity(nc, ident_bf16[:])

        one = const.tile([P, 1], F32)
        nc.vector.memset(one[:], 1.0)
        warm = const.tile([P, 1], F32)
        nc.scalar.activation(out=warm[:], in_=one[:], func=ACT.Abs_reciprocal_sqrt)

        g_rows = const.tile([P, P], BF16)
        nc.vector.memset(g_rows[:], 0.0)
        nc.sync.dma_start(out=g_rows[0:PACK, :], in_=g1.rearrange("(c p) -> c p", p=P))
        w_rows = const.tile([P, PACK, D], BF16)
        nc.sync.dma_start(out=w_rows[:], in_=wv.rearrange("(b p) k -> p b k", p=P))
        bias_rows = const.tile([P, D], BF16)
        nc.sync.dma_start(out=bias_rows[:], in_=bv.partition_broadcast(P))

        for g in range(VECTOR_ADDS):
            add_inputs(g)

        g_turned = turned.tile([P, PACK, P], BF16, tag="turned")
        nc.tensor.transpose(g_turned[:, 0, :], g_rows[:], ident_bf16[:])
        gain_by_k = const.tile([P, PACK], F32)
        nc.vector.tensor_copy(out=gain_by_k[:], in_=g_turned[:, 0, 0:PACK])

        w_words = const.tile([P, D, PACK], BF16, align_bytes=64)
        for b in range(PACK):
            w_turned = turned.tile([P, PACK, P], BF16, tag="turned")
            for c in range(PACK):
                nc.tensor.transpose(w_turned[:, c, :], w_rows[:, b, c * P : (c + 1) * P], ident_bf16[:])
            nc.vector.tensor_copy(
                out=w_words[:, b * P : (b + 1) * P, :], in_=w_turned[:].rearrange("p c n -> p n c")
            )
        w_codes = const.tile([P, D], U32, align_bytes=64)
        w_scales = const.tile([P, D], U8, align_bytes=64)
        nc.vector.quantize_mx(
            out=w_codes[:].bitcast(FP8X4), scales=w_scales[:], in_=w_words[:].rearrange("p n c -> p (n c)")
        )

        squares = const.tile([P, D], F32)

        def sum_squares(g, t):
            nc.scalar.activation(
                out=squares[:], in_=h[g][:, t, :], func=ACT.Square, accum_out=sum_sq[g][:, t : t + 1]
            )

        def clamp(g, t):
            nc.scalar.activation(
                out=excess[g][:, t : t + 1], in_=sum_sq[g][:, t : t + 1], func=ACT.Relu, bias=-EPS * EPS
            )

        def invert(g, t):
            nc.scalar.activation(
                out=inv_norm[g][:, t : t + 1],
                in_=excess[g][:, t : t + 1],
                func=ACT.Abs_reciprocal_sqrt,
                scale=float(D),
                bias=float(D) * EPS * EPS,
            )

        def scale_rows(g, t):
            nc.scalar.activation(
                out=h_unit[g][:, t, :], in_=h[g][:, t, :], func=ACT.Copy, scale=inv_norm[g][:, t : t + 1]
            )

        def normalise(g):
            sum_sq[g] = stats.tile([P, TILES], F32, name="sum_sq")
            excess[g] = stats.tile([P, TILES], F32, name="excess")
            inv_norm[g] = stats.tile([P, TILES], F32, name="inv_norm")
            h_unit[g] = scaled.tile([P, TILES, D], F32, name="h_unit")
            for i in range(2 * TILES):
                if i < TILES:
                    sum_squares(g, i)
                else:
                    scale_rows(g, i - TILES)
                if 1 <= i <= TILES:
                    clamp(g, i - 1)
                if 2 <= i <= TILES + 1:
                    invert(g, i - 2)

        def transpose(g):
            h_turned[g] = []
            for t in range(TILES):
                bank = turned.tile([P, PACK, P], F32, tag="turned", name="h_turned")
                for c in range(PACK):
                    nc.tensor.transpose(bank[:, c, :], h_unit[g][:, t, c * P : (c + 1) * P], ident_f32[:])
                h_turned[g].append(bank)

        def apply_gain(g):
            hn_words[g] = packed.tile([P, TILES, P, PACK], BF16, name="hn_words", align_bytes=64)
            for t in range(TILES):
                nc.vector.tensor_tensor(
                    out=hn_words[g][:, t, :, :],
                    in0=h_turned[g][t][:].rearrange("p c r -> p r c"),
                    in1=gain_by_k[:].unsqueeze(1).to_broadcast([P, P, PACK]),
                    op=ALU.mult,
                )

        def quantise(g):
            hn_codes[g] = packed.tile([P, TILES * P], U32, name="hn_codes", align_bytes=64)
            hn_scales[g] = packed.tile([P, TILES * P], U8, name="hn_scales", align_bytes=64)
            nc.vector.quantize_mx(
                out=hn_codes[g][:].bitcast(FP8X4),
                scales=hn_scales[g][:],
                in_=hn_words[g][:].rearrange("p t r c -> p (t r c)"),
            )

        def multiply(g):
            v_sums[g] = []
            for t in range(TILES):
                acc = products.tile([P, D], F32, tag="products", name="v_sums")
                nc.tensor.matmul_mx(
                    out=acc[:],
                    lhsT=hn_codes[g][:, t * P : (t + 1) * P].bitcast(FP8X4),
                    lhsT_scale=hn_scales[g][:, t * P : (t + 1) * P],
                    rhs=w_codes[:].bitcast(FP8X4),
                    rhs_scale=w_scales[:],
                    start=True,
                    stop=True,
                )
                v_sums[g].append(acc)

        def add_bias_and_store(g):
            v = results.tile([P, TILES, D], F32, name="v")
            for t in range(TILES):
                nc.vector.tensor_tensor(out=v[:, t, :], in0=v_sums[g][t][:], in1=bias_rows[:], op=ALU.add)
                if (t + 1) % STORE_TILES == 0:
                    part = slice(t + 1 - STORE_TILES, t + 1)
                    nc.sync.dma_start(out=group_view(out, g)[:, part, :], in_=v[:, part, :])

        def due(g):
            return 0 <= g < GROUPS

        for j in range(GROUPS + PRODUCT_LAG):
            if due(j + LOADS_AHEAD):
                load(j + LOADS_AHEAD)
            if VECTOR_ADDS <= j < GROUPS:
                add_inputs(j)
            if due(j - PRODUCT_LAG):
                quantise(j - PRODUCT_LAG)
                multiply(j - PRODUCT_LAG)
            if due(j - NORMALISE_LAG):
                normalise(j - NORMALISE_LAG)
                transpose(j - NORMALISE_LAG)
            if due(j - GAIN_LAG):
                apply_gain(j - GAIN_LAG)
            if due(j - PRODUCT_LAG):
                add_bias_and_store(j - PRODUCT_LAG)
